import numpy as np
import ml_dtypes


def mxq(x, axis, fmt="e4m3"):
    dtype, down = {"e4m3": (ml_dtypes.float8_e4m3fn, 7), "e5m2": (ml_dtypes.float8_e5m2, 14)}[fmt]
    v = np.moveaxis(np.asarray(x, np.float32).astype(ml_dtypes.bfloat16).astype(np.float64), axis, -1)
    blocks = v.reshape(v.shape[:-1] + (-1, 32))
    amax = np.abs(blocks).max(-1, keepdims=True)
    byte = np.maximum(np.where(amax > 0, np.frexp(amax)[1] - 1 + 127, 0) - down, 1)
    scale = np.exp2(byte - 127.0)
    codes = (blocks / scale).astype(np.float32).astype(dtype).astype(np.float64)
    return np.moveaxis((codes * scale).reshape(v.shape), -1, axis)


WIDE = False


def mx_kscale(k):
    if not WIDE:
        return np.ones(k)
    levels = np.array([10, -10, 5, -5, 0])
    a = np.random.permutation(np.resize(levels, k // 512 * 4)).reshape(k // 512, 4)
    idx = np.arange(k)
    return np.exp2(a[idx // 512, idx % 128 // 32])


BF16 = ml_dtypes.bfloat16


def bf(x):
    return np.asarray(x, np.float32).astype(BF16)


def f64(x):
    return np.asarray(x).astype(np.float64)


E2M1 = np.array([0.0, 0.5, 1.0, 1.5, 2.0, 3.0, 4.0, 6.0, -0.0, -0.5, -1.0, -1.5, -2.0, -3.0, -4.0, -6.0])


def pack_weight(w, fmt):
    k, n = w.shape
    w = f64(bf(w)).reshape(k // 32, 32, n)
    amax = np.abs(w).max(1)
    if fmt == "e4m3":
        byte = np.frexp(amax)[1] - 1 + 127 - 7
    else:
        mant, ex = np.frexp(amax / 6.0)
        byte = np.where(mant > 0.5, ex, ex - 1) + 127
    byte = np.clip(np.where(amax > 0, byte, 1), 1, 254)
    scaled = (w * np.exp2(127.0 - byte)[:, None, :]).reshape(k, n).astype(np.float32)
    by_word = np.ascontiguousarray(scaled.reshape(k // 512, 128, 4, n).transpose(0, 1, 3, 2))
    if fmt == "e4m3":
        words = by_word.astype(ml_dtypes.float8_e4m3fn).view(np.uint8)
    else:
        c = by_word.astype(ml_dtypes.float4_e2m1fn).view(np.uint8) & 0xF
        words = c[..., 0::2] | (c[..., 1::2] << 4)
    return np.ascontiguousarray(words), np.ascontiguousarray(byte.astype(np.uint8).reshape(k // 512, 16, n))


def unpack_weight(words, scales, fmt):
    g, p, n, _ = words.shape
    if fmt == "e4m3":
        vals = np.ascontiguousarray(words).view(ml_dtypes.float8_e4m3fn).astype(np.float64)
    else:
        nib = np.empty((g, p, n, 4), np.uint8)
        nib[..., 0::2] = words & 0xF
        nib[..., 1::2] = words >> 4
        vals = E2M1[nib]
    vals = vals * np.repeat(np.exp2(scales.astype(np.float64) - 127.0), 8, axis=1)[..., None]
    return vals.transpose(0, 1, 3, 2).reshape(g * 512, n)


B, T, E, Q = 4, 4096, 128, 512
N = B * T


def setup_inputs():
    s = mx_kscale(Q)
    y = bf(np.random.standard_normal((B, T, Q)) * s)
    w = np.random.standard_normal((2 * E, Q)) / np.sqrt(Q) / s
    words, scales = pack_weight(np.ascontiguousarray(w.T), "e4m3")
    return {"y": y, "w_swiglu_words": words, "w_swiglu_scales": scales}


def reference(y, w_swiglu_words, w_swiglu_scales):
    uv = mxq(f64(y).reshape(N, Q), 1, "e4m3") @ unpack_weight(w_swiglu_words, w_swiglu_scales, "e4m3")
    u, v = uv[:, :E], uv[:, E:]
    ao = mxq(u.T, 1, "e4m3") @ mxq(v, 0, "e4m3")
    return ao / B * E ** (-0.5)

@@ -1,0 +1,158 @@
+from contextlib import ExitStack
+import math
+
+import concourse.mybir as mybir
+from concourse.masks import make_identity
+
+F32 = mybir.dt.float32
+BF16 = mybir.dt.bfloat16
+I32 = mybir.dt.int32
+U32 = mybir.dt.uint32
+U8 = mybir.dt.uint8
+FP8X4 = mybir.dt.float8_e4m3fn_x4
+
+P = 128
+PACK = 4
+K_PASS = P * PACK
+
+BATCH, TOKENS, FEATURES, WIDTH = 4, 4096, 512, 128
+ALL_TOKENS = BATCH * TOKENS
+GROUPS = ALL_TOKENS // K_PASS
+WORDS = FEATURES // 2
+
+FLOPS = 2 * ALL_TOKENS * FEATURES * 2 * WIDTH + 2 * ALL_TOKENS * WIDTH * WIDTH
+
+
+def tile_retentionmechanism_pa_t_kernel(tc, y, w_swiglu_words, w_swiglu_scales, out):
+    nc = tc.nc
+    assert FEATURES == K_PASS
+
+    y_groups = y.rearrange("b t q -> (b t) q").rearrange("(g p j) q -> g p (j q)", p=P, j=PACK)
+
+    with ExitStack() as ctx:
+        ctx.enter_context(tc.manual_schedule())
+        consts = ctx.enter_context(tc.tile_pool(name="consts", bufs=1))
+        y_pool = ctx.enter_context(tc.tile_pool(name="y_pool", bufs=GROUPS))
+        work = ctx.enter_context(tc.tile_pool(name="work", bufs=3))
+        psum_t = ctx.enter_context(tc.psum_pool(name="psum_t", bufs=4))
+        psum_uv = ctx.enter_context(tc.psum_pool(name="psum_uv", bufs=3))
+        psum_out = ctx.enter_context(tc.psum_pool(name="psum_out", bufs=1))
+
+        identity = consts.tile([P, P], F32)
+        make_identity(nc, identity[:])
+
+        w_codes = consts.tile([P, 2 * WIDTH], U32, align_bytes=64)
+        w_scales = consts.tile([P, 2 * WIDTH], U8, align_bytes=64)
+        nc.vector.memset(w_scales[:].bitcast(I32), 0)
+
+        y_tiles = []
+        for g in range(GROUPS):
+            y_sb = y_pool.tile([P, PACK * FEATURES], BF16, name="y_sb")
+            nc.sync.dma_start(out=y_sb[:], in_=y_groups[g])
+            y_tiles.append(y_sb)
+            if g == 0:
+                nc.sync.dma_start(
+                    out=w_codes[:].bitcast(I32),
+                    in_=w_swiglu_words.rearrange("g p n t -> (g p) (n t)").bitcast(I32),
+                )
+                for r in range(4):
+                    nc.sync.dma_start(
+                        out=w_scales[r:P:32, :].bitcast(I32),
+                        in_=w_swiglu_scales[0, r:16:4, :].bitcast(I32),
+                    )
+
+        result = psum_out.tile([P, WIDTH], F32)
+        y_grouped, y_codes, y_scales = {}, {}, {}
+        uv_banks, uv_grouped, uv_codes, uv_scales = {}, {}, {}, {}
+
+        def transpose_group(g):
+            y_words = y_tiles[g][:].bitcast(F32)
+            y_grouped[g] = work.tile([P, PACK * K_PASS], BF16, name="y_grouped", align_bytes=64)
+            grouped_words = y_grouped[g][:].bitcast(F32)
+            for b in range(2):
+                bank = psum_t.tile([P, 2, 2, P], F32, name="bank_t")
+                for a in range(2):
+                    j = 2 * b + a
+                    for u in range(2):
+                        nc.tensor.transpose(
+                            bank[:, a, u, :],
+                            y_words[:, WORDS * j + u : WORDS * (j + 1) : 2],
+                            identity[:],
+                        )
+                nc.scalar.copy(
+                    out=grouped_words[:, 4 * P * b : 4 * P * (b + 1)].rearrange(
+                        "p (a r u) -> p a r u", a=2, u=2
+                    ),
+                    in_=bank[:].rearrange("p a u r -> p a r u"),
+                )
+
+        def quantise_y(g):
+            y_codes[g] = work.tile([P, K_PASS], U32, name="y_codes", align_bytes=64)
+            y_scales[g] = work.tile([P, K_PASS], U8, name="y_scales", align_bytes=64)
+            nc.vector.quantize_mx(
+                out=y_codes[g][:].bitcast(FP8X4), scales=y_scales[g][:], in_=y_grouped[g][:]
+            )
+
+        def first_product(g):
+            for half in range(2):
+                columns = slice(WIDTH * half, WIDTH * (half + 1))
+                bank = psum_uv.tile([P, PACK, WIDTH], F32, name="bank_uv")
+                for j in range(PACK):
+                    tokens = slice(P * j, P * (j + 1))
+                    nc.tensor.matmul_mx(
+                        out=bank[:, j, :],
+                        lhsT=y_codes[g][:, tokens].bitcast(FP8X4),
+                        lhsT_scale=y_scales[g][:, tokens],
+                        rhs=w_codes[:, columns].bitcast(FP8X4),
+                        rhs_scale=w_scales[:, columns],
+                        start=True,
+                        stop=True,
+                    )
+                uv_banks[(g, half)] = bank
+            uv_grouped[g] = work.tile([P, 2 * WIDTH, PACK], BF16, name="uv_grouped", align_bytes=64)
+
+        def round_half(g, half, copy):
+            copy(
+                out=uv_grouped[g][:, WIDTH * half : WIDTH * (half + 1), :],
+                in_=uv_banks[(g, half)][:].rearrange("p j w -> p w j"),
+            )
+
+        def quantise_uv(g):
+            uv_codes[g] = work.tile([P, 2 * WIDTH], U32, name="uv_codes", align_bytes=64)
+            uv_scales[g] = work.tile([P, 2 * WIDTH], U8, name="uv_scales", align_bytes=64)
+            nc.vector.quantize_mx(
+                out=uv_codes[g][:].bitcast(FP8X4),
+                scales=uv_scales[g][:],
+                in_=uv_grouped[g][:].rearrange("p w j -> p (w j)"),
+            )
+
+        def second_product(g):
+            nc.tensor.matmul_mx(
+                out=result[:],
+                lhsT=uv_codes[g][:, 0:WIDTH].bitcast(FP8X4),
+                lhsT_scale=uv_scales[g][:, 0:WIDTH],
+                rhs=uv_codes[g][:, WIDTH : 2 * WIDTH].bitcast(FP8X4),
+                rhs_scale=uv_scales[g][:, WIDTH : 2 * WIDTH],
+                start=(g == 0),
+                stop=(g == GROUPS - 1),
+            )
+
+        for i in range(GROUPS + 3):
+            if i < GROUPS:
+                transpose_group(i)
+            if 0 <= i - 1 < GROUPS:
+                first_product(i - 1)
+            if 0 <= i - 3 < GROUPS:
+                second_product(i - 3)
+            if 0 <= i - 1 < GROUPS:
+                round_half(i - 1, 0, nc.scalar.copy)
+            if i < GROUPS:
+                quantise_y(i)
+            if 0 <= i - 2 < GROUPS:
+                quantise_uv(i - 2)
+            if 0 <= i - 1 < GROUPS:
+                round_half(i - 1, 1, nc.vector.tensor_copy)
+
+        scaled = consts.tile([P, WIDTH], F32)
+        nc.vector.tensor_scalar_mul(out=scaled[:], in0=result[:], scalar1=1.0 / BATCH / math.sqrt(WIDTH))
+        nc.sync.dma_start(out=out, in_=scaled[:])

@@ -19,6 +19,7 @@ BATCH, TOKENS, FEATURES, WIDTH = 4, 4096, 512, 128
 ALL_TOKENS = BATCH * TOKENS
 GROUPS = ALL_TOKENS // K_PASS
 WORDS = FEATURES // 2
+Y_BUFFERS = 8
 
 FLOPS = 2 * ALL_TOKENS * FEATURES * 2 * WIDTH + 2 * ALL_TOKENS * WIDTH * WIDTH
 
@@ -32,10 +33,10 @@ def tile_retentionmechanism_pa_t_kernel(tc, y, w_swiglu_words, w_swiglu_scales, 
     with ExitStack() as ctx:
         ctx.enter_context(tc.manual_schedule())
         consts = ctx.enter_context(tc.tile_pool(name="consts", bufs=1))
-        y_pool = ctx.enter_context(tc.tile_pool(name="y_pool", bufs=GROUPS))
-        work = ctx.enter_context(tc.tile_pool(name="work", bufs=3))
-        psum_t = ctx.enter_context(tc.psum_pool(name="psum_t", bufs=4))
-        psum_uv = ctx.enter_context(tc.psum_pool(name="psum_uv", bufs=3))
+        y_pool = ctx.enter_context(tc.tile_pool(name="y_pool", bufs=Y_BUFFERS))
+        keep = ctx.enter_context(tc.tile_pool(name="keep", bufs=GROUPS))
+        work = ctx.enter_context(tc.tile_pool(name="work", bufs=4))
+        psum = ctx.enter_context(tc.psum_pool(name="psum", bufs=7))
         psum_out = ctx.enter_context(tc.psum_pool(name="psum_out", bufs=1))
 
         identity = consts.tile([P, P], F32)
@@ -45,32 +46,30 @@ def tile_retentionmechanism_pa_t_kernel(tc, y, w_swiglu_words, w_swiglu_scales, 
         w_scales = consts.tile([P, 2 * WIDTH], U8, align_bytes=64)
         nc.vector.memset(w_scales[:].bitcast(I32), 0)
 
-        y_tiles = []
-        for g in range(GROUPS):
-            y_sb = y_pool.tile([P, PACK * FEATURES], BF16, name="y_sb")
-            nc.sync.dma_start(out=y_sb[:], in_=y_groups[g])
-            y_tiles.append(y_sb)
-            if g == 0:
-                nc.sync.dma_start(
-                    out=w_codes[:].bitcast(I32),
-                    in_=w_swiglu_words.rearrange("g p n t -> (g p) (n t)").bitcast(I32),
-                )
-                for r in range(4):
-                    nc.sync.dma_start(
-                        out=w_scales[r:P:32, :].bitcast(I32),
-                        in_=w_swiglu_scales[0, r:16:4, :].bitcast(I32),
-                    )
-
-        result = psum_out.tile([P, WIDTH], F32)
-        y_grouped, y_codes, y_scales = {}, {}, {}
+        y_tiles, y_grouped, y_codes, y_scales = {}, {}, {}, {}
         uv_banks, uv_grouped, uv_codes, uv_scales = {}, {}, {}, {}
+
+        def load_group(g):
+            y_tiles[g] = y_pool.tile([P, PACK * FEATURES], BF16, name="y_sb")
+            nc.sync.dma_start(out=y_tiles[g][:], in_=y_groups[g])
+
+        def load_w():
+            nc.sync.dma_start(
+                out=w_codes[:].bitcast(I32),
+                in_=w_swiglu_words.rearrange("g p n t -> (g p) (n t)").bitcast(I32),
+            )
+            for r in range(4):
+                nc.sync.dma_start(
+                    out=w_scales[r:P:32, :].bitcast(I32),
+                    in_=w_swiglu_scales[0, r:16:4, :].bitcast(I32),
+                )
 
         def transpose_group(g):
             y_words = y_tiles[g][:].bitcast(F32)
             y_grouped[g] = work.tile([P, PACK * K_PASS], BF16, name="y_grouped", align_bytes=64)
             grouped_words = y_grouped[g][:].bitcast(F32)
             for b in range(2):
-                bank = psum_t.tile([P, 2, 2, P], F32, name="bank_t")
+                bank = psum.tile([P, 2, 2, P], F32, name="bank_t", tag="bank")
                 for a in range(2):
                     j = 2 * b + a
                     for u in range(2):
@@ -79,7 +78,8 @@ def tile_retentionmechanism_pa_t_kernel(tc, y, w_swiglu_words, w_swiglu_scales, 
                             y_words[:, WORDS * j + u : WORDS * (j + 1) : 2],
                             identity[:],
                         )
-                nc.scalar.copy(
+                copy = nc.vector.tensor_copy if (2 * g + b) % 4 == 3 else nc.scalar.copy
+                copy(
                     out=grouped_words[:, 4 * P * b : 4 * P * (b + 1)].rearrange(
                         "p (a r u) -> p a r u", a=2, u=2
                     ),
@@ -87,8 +87,8 @@ def tile_retentionmechanism_pa_t_kernel(tc, y, w_swiglu_words, w_swiglu_scales, 
                 )
 
         def quantise_y(g):
-            y_codes[g] = work.tile([P, K_PASS], U32, name="y_codes", align_bytes=64)
-            y_scales[g] = work.tile([P, K_PASS], U8, name="y_scales", align_bytes=64)
+            y_codes[g] = keep.tile([P, K_PASS], U32, name="y_codes", align_bytes=64)
+            y_scales[g] = keep.tile([P, K_PASS], U8, name="y_scales", align_bytes=64)
             nc.vector.quantize_mx(
                 out=y_codes[g][:].bitcast(FP8X4), scales=y_scales[g][:], in_=y_grouped[g][:]
             )
@@ -96,7 +96,7 @@ def tile_retentionmechanism_pa_t_kernel(tc, y, w_swiglu_words, w_swiglu_scales, 
         def first_product(g):
             for half in range(2):
                 columns = slice(WIDTH * half, WIDTH * (half + 1))
-                bank = psum_uv.tile([P, PACK, WIDTH], F32, name="bank_uv")
+                bank = psum.tile([P, PACK, WIDTH], F32, name="bank_uv", tag="bank")
                 for j in range(PACK):
                     tokens = slice(P * j, P * (j + 1))
                     nc.tensor.matmul_mx(
@@ -109,13 +109,15 @@ def tile_retentionmechanism_pa_t_kernel(tc, y, w_swiglu_words, w_swiglu_scales, 
                         stop=True,
                     )
                 uv_banks[(g, half)] = bank
-            uv_grouped[g] = work.tile([P, 2 * WIDTH, PACK], BF16, name="uv_grouped", align_bytes=64)
 
-        def round_half(g, half, copy):
-            copy(
-                out=uv_grouped[g][:, WIDTH * half : WIDTH * (half + 1), :],
-                in_=uv_banks[(g, half)][:].rearrange("p j w -> p w j"),
-            )
+        def round_uv(g):
+            uv_grouped[g] = work.tile([P, 2 * WIDTH, PACK], BF16, name="uv_grouped", align_bytes=64)
+            for half in range(2):
+                copy = nc.vector.tensor_copy if (half == 1 and g % 4 != 3) else nc.scalar.copy
+                copy(
+                    out=uv_grouped[g][:, WIDTH * half : WIDTH * (half + 1), :],
+                    in_=uv_banks[(g, half)][:].rearrange("p j w -> p w j"),
+                )
 
         def quantise_uv(g):
             uv_codes[g] = work.tile([P, 2 * WIDTH], U32, name="uv_codes", align_bytes=64)
@@ -137,21 +139,28 @@ def tile_retentionmechanism_pa_t_kernel(tc, y, w_swiglu_words, w_swiglu_scales, 
                 stop=(g == GROUPS - 1),
             )
 
-        for i in range(GROUPS + 3):
-            if i < GROUPS:
-                transpose_group(i)
-            if 0 <= i - 1 < GROUPS:
-                first_product(i - 1)
-            if 0 <= i - 3 < GROUPS:
-                second_product(i - 3)
-            if 0 <= i - 1 < GROUPS:
-                round_half(i - 1, 0, nc.scalar.copy)
-            if i < GROUPS:
-                quantise_y(i)
-            if 0 <= i - 2 < GROUPS:
-                quantise_uv(i - 2)
-            if 0 <= i - 1 < GROUPS:
-                round_half(i - 1, 1, nc.vector.tensor_copy)
+        for g in range(Y_BUFFERS):
+            load_group(g)
+            if g == 0:
+                load_w()
+        for g in range(GROUPS + 2):
+            if g >= 2:
+                quantise_y(g - 2)
+            if g < GROUPS:
+                transpose_group(g)
+            if g + Y_BUFFERS < GROUPS:
+                load_group(g + Y_BUFFERS)
+
+        result = psum_out.tile([P, WIDTH], F32)
+        for g in range(GROUPS + 2):
+            if g < GROUPS:
+                first_product(g)
+            if g >= 2:
+                second_product(g - 2)
+            if g < GROUPS:
+                round_uv(g)
+            if 1 <= g <= GROUPS:
+                quantise_uv(g - 1)
 
         scaled = consts.tile([P, WIDTH], F32)
         nc.vector.tensor_scalar_mul(out=scaled[:], in0=result[:], scalar1=1.0 / BATCH / math.sqrt(WIDTH))

@@ -20,6 +20,7 @@ ALL_TOKENS = BATCH * TOKENS
 GROUPS = ALL_TOKENS // K_PASS
 WORDS = FEATURES // 2
 Y_BUFFERS = 8
+SECOND_LAG = 4
 
 FLOPS = 2 * ALL_TOKENS * FEATURES * 2 * WIDTH + 2 * ALL_TOKENS * WIDTH * WIDTH
 
@@ -36,6 +37,7 @@ def tile_retentionmechanism_pa_t_kernel(tc, y, w_swiglu_words, w_swiglu_scales, 
         y_pool = ctx.enter_context(tc.tile_pool(name="y_pool", bufs=Y_BUFFERS))
         keep = ctx.enter_context(tc.tile_pool(name="keep", bufs=GROUPS))
         work = ctx.enter_context(tc.tile_pool(name="work", bufs=4))
+        uv_pool = ctx.enter_context(tc.tile_pool(name="uv_pool", bufs=SECOND_LAG + 1))
         psum = ctx.enter_context(tc.psum_pool(name="psum", bufs=7))
         psum_out = ctx.enter_context(tc.psum_pool(name="psum_out", bufs=1))
 
@@ -113,15 +115,15 @@ def tile_retentionmechanism_pa_t_kernel(tc, y, w_swiglu_words, w_swiglu_scales, 
         def round_uv(g):
             uv_grouped[g] = work.tile([P, 2 * WIDTH, PACK], BF16, name="uv_grouped", align_bytes=64)
             for half in range(2):
-                copy = nc.vector.tensor_copy if (half == 1 and g % 4 != 3) else nc.scalar.copy
+                copy = nc.vector.tensor_copy if (2 * g + half) % 3 == 2 else nc.scalar.copy
                 copy(
                     out=uv_grouped[g][:, WIDTH * half : WIDTH * (half + 1), :],
                     in_=uv_banks[(g, half)][:].rearrange("p j w -> p w j"),
                 )
 
         def quantise_uv(g):
-            uv_codes[g] = work.tile([P, 2 * WIDTH], U32, name="uv_codes", align_bytes=64)
-            uv_scales[g] = work.tile([P, 2 * WIDTH], U8, name="uv_scales", align_bytes=64)
+            uv_codes[g] = uv_pool.tile([P, 2 * WIDTH], U32, name="uv_codes", align_bytes=64)
+            uv_scales[g] = uv_pool.tile([P, 2 * WIDTH], U8, name="uv_scales", align_bytes=64)
             nc.vector.quantize_mx(
                 out=uv_codes[g][:].bitcast(FP8X4),
                 scales=uv_scales[g][:],
@@ -152,11 +154,11 @@ def tile_retentionmechanism_pa_t_kernel(tc, y, w_swiglu_words, w_swiglu_scales, 
                 load_group(g + Y_BUFFERS)
 
         result = psum_out.tile([P, WIDTH], F32)
-        for g in range(GROUPS + 2):
+        for g in range(GROUPS + SECOND_LAG):
             if g < GROUPS:
                 first_product(g)
-            if g >= 2:
-                second_product(g - 2)
+            if g >= SECOND_LAG:
+                second_product(g - SECOND_LAG)
             if g < GROUPS:
                 round_uv(g)
             if 1 <= g <= GROUPS:

@@ -18,9 +18,10 @@ K_PASS = P * PACK
 BATCH, TOKENS, FEATURES, WIDTH = 4, 4096, 512, 128
 ALL_TOKENS = BATCH * TOKENS
 GROUPS = ALL_TOKENS // K_PASS
+PER_ROUND = 2
+ROUNDS = GROUPS // PER_ROUND
 WORDS = FEATURES // 2
 Y_BUFFERS = 8
-SECOND_LAG = 4
 
 FLOPS = 2 * ALL_TOKENS * FEATURES * 2 * WIDTH + 2 * ALL_TOKENS * WIDTH * WIDTH
 
@@ -35,11 +36,10 @@ def tile_retentionmechanism_pa_t_kernel(tc, y, w_swiglu_words, w_swiglu_scales, 
         ctx.enter_context(tc.manual_schedule())
         consts = ctx.enter_context(tc.tile_pool(name="consts", bufs=1))
         y_pool = ctx.enter_context(tc.tile_pool(name="y_pool", bufs=Y_BUFFERS))
-        keep = ctx.enter_context(tc.tile_pool(name="keep", bufs=GROUPS))
-        work = ctx.enter_context(tc.tile_pool(name="work", bufs=4))
-        uv_pool = ctx.enter_context(tc.tile_pool(name="uv_pool", bufs=SECOND_LAG + 1))
-        psum = ctx.enter_context(tc.psum_pool(name="psum", bufs=7))
-        psum_out = ctx.enter_context(tc.psum_pool(name="psum_out", bufs=1))
+        work = ctx.enter_context(tc.tile_pool(name="work", bufs=6))
+        uv_pool = ctx.enter_context(tc.tile_pool(name="uv_pool", bufs=GROUPS))
+        psum_t = ctx.enter_context(tc.psum_pool(name="psum_t", bufs=4))
+        psum_m = ctx.enter_context(tc.psum_pool(name="psum_m", bufs=4))
 
         identity = consts.tile([P, P], F32)
         make_identity(nc, identity[:])
@@ -49,7 +49,7 @@ def tile_retentionmechanism_pa_t_kernel(tc, y, w_swiglu_words, w_swiglu_scales, 
         nc.vector.memset(w_scales[:].bitcast(I32), 0)
 
         y_tiles, y_grouped, y_codes, y_scales = {}, {}, {}, {}
-        uv_banks, uv_grouped, uv_codes, uv_scales = {}, {}, {}, {}
+        t_banks, m_banks, uv_grouped, uv_codes, uv_scales = {}, {}, {}, {}, {}
 
         def load_group(g):
             y_tiles[g] = y_pool.tile([P, PACK * FEATURES], BF16, name="y_sb")
@@ -66,31 +66,32 @@ def tile_retentionmechanism_pa_t_kernel(tc, y, w_swiglu_words, w_swiglu_scales, 
                     in_=w_swiglu_scales[0, r:16:4, :].bitcast(I32),
                 )
 
-        def transpose_group(g):
+        def transpose_bank(g, b):
             y_words = y_tiles[g][:].bitcast(F32)
-            y_grouped[g] = work.tile([P, PACK * K_PASS], BF16, name="y_grouped", align_bytes=64)
-            grouped_words = y_grouped[g][:].bitcast(F32)
-            for b in range(2):
-                bank = psum.tile([P, 2, 2, P], F32, name="bank_t", tag="bank")
-                for a in range(2):
-                    j = 2 * b + a
-                    for u in range(2):
-                        nc.tensor.transpose(
-                            bank[:, a, u, :],
-                            y_words[:, WORDS * j + u : WORDS * (j + 1) : 2],
-                            identity[:],
-                        )
-                copy = nc.vector.tensor_copy if (2 * g + b) % 4 == 3 else nc.scalar.copy
-                copy(
-                    out=grouped_words[:, 4 * P * b : 4 * P * (b + 1)].rearrange(
-                        "p (a r u) -> p a r u", a=2, u=2
-                    ),
-                    in_=bank[:].rearrange("p a u r -> p a r u"),
-                )
+            bank = psum_t.tile([P, 2, 2, P], F32, name="bank_t")
+            for a in range(2):
+                j = 2 * b + a
+                for u in range(2):
+                    nc.tensor.transpose(
+                        bank[:, a, u, :],
+                        y_words[:, WORDS * j + u : WORDS * (j + 1) : 2],
+                        identity[:],
+                    )
+            t_banks[(g, b)] = bank
+
+        def copy_t(copy, g, b):
+            if b == 0:
+                y_grouped[g] = work.tile([P, PACK * K_PASS], BF16, name="y_grouped", align_bytes=64)
+            copy(
+                out=y_grouped[g][:].bitcast(F32)[:, 4 * P * b : 4 * P * (b + 1)].rearrange(
+                    "p (a r u) -> p a r u", a=2, u=2
+                ),
+                in_=t_banks[(g, b)][:].rearrange("p a u r -> p a r u"),
+            )
 
         def quantise_y(g):
-            y_codes[g] = keep.tile([P, K_PASS], U32, name="y_codes", align_bytes=64)
-            y_scales[g] = keep.tile([P, K_PASS], U8, name="y_scales", align_bytes=64)
+            y_codes[g] = work.tile([P, K_PASS], U32, name="y_codes", align_bytes=64)
+            y_scales[g] = work.tile([P, K_PASS], U8, name="y_scales", align_bytes=64)
             nc.vector.quantize_mx(
                 out=y_codes[g][:].bitcast(FP8X4), scales=y_scales[g][:], in_=y_grouped[g][:]
             )
@@ -98,7 +99,7 @@ def tile_retentionmechanism_pa_t_kernel(tc, y, w_swiglu_words, w_swiglu_scales, 
         def first_product(g):
             for half in range(2):
                 columns = slice(WIDTH * half, WIDTH * (half + 1))
-                bank = psum.tile([P, PACK, WIDTH], F32, name="bank_uv", tag="bank")
+                bank = psum_m.tile([P, PACK, WIDTH], F32, name="bank_m")
                 for j in range(PACK):
                     tokens = slice(P * j, P * (j + 1))
                     nc.tensor.matmul_mx(
@@ -110,16 +111,15 @@ def tile_retentionmechanism_pa_t_kernel(tc, y, w_swiglu_words, w_swiglu_scales, 
                         start=True,
                         stop=True,
                     )
-                uv_banks[(g, half)] = bank
+                m_banks[(g, half)] = bank
 
-        def round_uv(g):
-            uv_grouped[g] = work.tile([P, 2 * WIDTH, PACK], BF16, name="uv_grouped", align_bytes=64)
-            for half in range(2):
-                copy = nc.vector.tensor_copy if (2 * g + half) % 3 == 2 else nc.scalar.copy
-                copy(
-                    out=uv_grouped[g][:, WIDTH * half : WIDTH * (half + 1), :],
-                    in_=uv_banks[(g, half)][:].rearrange("p j w -> p w j"),
-                )
+        def copy_m(copy, g, half):
+            if half == 0:
+                uv_grouped[g] = work.tile([P, 2 * WIDTH, PACK], BF16, name="uv_grouped", align_bytes=64)
+            copy(
+                out=uv_grouped[g][:, WIDTH * half : WIDTH * (half + 1), :],
+                in_=m_banks[(g, half)][:].rearrange("p j w -> p w j"),
+            )
 
         def quantise_uv(g):
             uv_codes[g] = uv_pool.tile([P, 2 * WIDTH], U32, name="uv_codes", align_bytes=64)
@@ -132,7 +132,7 @@ def tile_retentionmechanism_pa_t_kernel(tc, y, w_swiglu_words, w_swiglu_scales, 
 
         def second_product(g):
             nc.tensor.matmul_mx(
-                out=result[:],
+                out=result,
                 lhsT=uv_codes[g][:, 0:WIDTH].bitcast(FP8X4),
                 lhsT_scale=uv_scales[g][:, 0:WIDTH],
                 rhs=uv_codes[g][:, WIDTH : 2 * WIDTH].bitcast(FP8X4),
@@ -141,29 +141,49 @@ def tile_retentionmechanism_pa_t_kernel(tc, y, w_swiglu_words, w_swiglu_scales, 
                 stop=(g == GROUPS - 1),
             )
 
+        s_copy, v_copy = nc.scalar.copy, nc.vector.tensor_copy
+
         for g in range(Y_BUFFERS):
             load_group(g)
-            if g == 0:
+            if g == 3:
                 load_w()
-        for g in range(GROUPS + 2):
-            if g >= 2:
-                quantise_y(g - 2)
-            if g < GROUPS:
-                transpose_group(g)
-            if g + Y_BUFFERS < GROUPS:
-                load_group(g + Y_BUFFERS)
 
-        result = psum_out.tile([P, WIDTH], F32)
-        for g in range(GROUPS + SECOND_LAG):
-            if g < GROUPS:
-                first_product(g)
-            if g >= SECOND_LAG:
-                second_product(g - SECOND_LAG)
-            if g < GROUPS:
-                round_uv(g)
-            if 1 <= g <= GROUPS:
-                quantise_uv(g - 1)
+        for r in range(ROUNDS + 3):
+            now = [PER_ROUND * r + i for i in range(PER_ROUND)]
+            one = [g - PER_ROUND for g in now]
+            two = [g - 2 * PER_ROUND for g in now]
+            three = [g - 3 * PER_ROUND for g in now]
+            if r < ROUNDS:
+                for g in now:
+                    for b in range(2):
+                        transpose_bank(g, b)
+                    if g + Y_BUFFERS < GROUPS:
+                        load_group(g + Y_BUFFERS)
+            if 2 <= r < ROUNDS + 2:
+                copy_m(s_copy, two[0], 0)
+                copy_m(v_copy, two[0], 1)
+                copy_m(s_copy, two[1], 0)
+                copy_m(s_copy, two[1], 1)
+            if 1 <= r < ROUNDS + 1:
+                for g in one:
+                    quantise_y(g)
+                for g in one:
+                    first_product(g)
+            if r < ROUNDS:
+                copy_t(s_copy, now[0], 0)
+                copy_t(s_copy, now[0], 1)
+                copy_t(v_copy, now[1], 0)
+                copy_t(v_copy if r % 4 == 3 else s_copy, now[1], 1)
+            if r >= 3:
+                for g in three:
+                    quantise_uv(g)
+            if r == ROUNDS - 1:
+                result = psum_t.tile([P, 2, 2, P], F32, name="bank_t")[:, 0, 0, :]
+                for g in range(GROUPS // 2):
+                    second_product(g)
+        for g in range(GROUPS // 2, GROUPS):
+            second_product(g)
 
         scaled = consts.tile([P, WIDTH], F32)
-        nc.vector.tensor_scalar_mul(out=scaled[:], in0=result[:], scalar1=1.0 / BATCH / math.sqrt(WIDTH))
+        nc.vector.tensor_scalar_mul(out=scaled[:], in0=result, scalar1=1.0 / BATCH / math.sqrt(WIDTH))
         nc.sync.dma_start(out=out, in_=scaled[:])

@@ -36,6 +36,7 @@ def tile_retentionmechanism_pa_t_kernel(tc, y, w_swiglu_words, w_swiglu_scales, 
         ctx.enter_context(tc.manual_schedule())
         consts = ctx.enter_context(tc.tile_pool(name="consts", bufs=1))
         y_pool = ctx.enter_context(tc.tile_pool(name="y_pool", bufs=Y_BUFFERS))
+        ordered_pool = ctx.enter_context(tc.tile_pool(name="ordered_pool", bufs=3))
         work = ctx.enter_context(tc.tile_pool(name="work", bufs=6))
         uv_pool = ctx.enter_context(tc.tile_pool(name="uv_pool", bufs=GROUPS))
         psum_t = ctx.enter_context(tc.psum_pool(name="psum_t", bufs=4))
@@ -48,7 +49,7 @@ def tile_retentionmechanism_pa_t_kernel(tc, y, w_swiglu_words, w_swiglu_scales, 
         w_scales = consts.tile([P, 2 * WIDTH], U8, align_bytes=64)
         nc.vector.memset(w_scales[:].bitcast(I32), 0)
 
-        y_tiles, y_grouped, y_codes, y_scales = {}, {}, {}, {}
+        y_tiles, y_ordered, y_grouped, y_codes, y_scales = {}, {}, {}, {}, {}
         t_banks, m_banks, uv_grouped, uv_codes, uv_scales = {}, {}, {}, {}, {}
 
         def load_group(g):
@@ -66,17 +67,26 @@ def tile_retentionmechanism_pa_t_kernel(tc, y, w_swiglu_words, w_swiglu_scales, 
                     in_=w_swiglu_scales[0, r:16:4, :].bitcast(I32),
                 )
 
+        def order_group(g):
+            y_ordered[g] = ordered_pool.tile([P, PACK * WORDS], F32, name="y_ordered")
+            for half in range(2):
+                columns = slice(2 * WORDS * half, 2 * WORDS * (half + 1))
+                nc.gpsimd.tensor_copy(
+                    out=y_ordered[g][:, columns].rearrange("p (j u c) -> p j u c", j=2, u=2),
+                    in_=y_tiles[g][:].bitcast(F32)[:, columns].rearrange("p (j c u) -> p j u c", j=2, u=2),
+                )
+
+        def word_columns(g, j, u):
+            if g in y_ordered:
+                return y_ordered[g][:, WORDS * j + P * u : WORDS * j + P * (u + 1)]
+            return y_tiles[g][:].bitcast(F32)[:, WORDS * j + u : WORDS * (j + 1) : 2]
+
         def transpose_bank(g, b):
-            y_words = y_tiles[g][:].bitcast(F32)
             bank = psum_t.tile([P, 2, 2, P], F32, name="bank_t")
             for a in range(2):
                 j = 2 * b + a
                 for u in range(2):
-                    nc.tensor.transpose(
-                        bank[:, a, u, :],
-                        y_words[:, WORDS * j + u : WORDS * (j + 1) : 2],
-                        identity[:],
-                    )
+                    nc.tensor.transpose(bank[:, a, u, :], word_columns(g, j, u), identity[:])
             t_banks[(g, b)] = bank
 
         def copy_t(copy, g, b):
@@ -169,6 +179,8 @@ def tile_retentionmechanism_pa_t_kernel(tc, y, w_swiglu_words, w_swiglu_scales, 
                     quantise_y(g)
                 for g in one:
                     first_product(g)
+            if r % 2 == 0 and r + 2 < ROUNDS:
+                order_group(PER_ROUND * (r + 2) + 1)
             if r < ROUNDS:
                 copy_t(s_copy, now[0], 0)
                 copy_t(s_copy, now[0], 1)

@@ -18,8 +18,6 @@ K_PASS = P * PACK
 BATCH, TOKENS, FEATURES, WIDTH = 4, 4096, 512, 128
 ALL_TOKENS = BATCH * TOKENS
 GROUPS = ALL_TOKENS // K_PASS
-PER_ROUND = 2
-ROUNDS = GROUPS // PER_ROUND
 WORDS = FEATURES // 2
 Y_BUFFERS = 8
 
@@ -36,7 +34,7 @@ def tile_retentionmechanism_pa_t_kernel(tc, y, w_swiglu_words, w_swiglu_scales, 
         ctx.enter_context(tc.manual_schedule())
         consts = ctx.enter_context(tc.tile_pool(name="consts", bufs=1))
         y_pool = ctx.enter_context(tc.tile_pool(name="y_pool", bufs=Y_BUFFERS))
-        ordered_pool = ctx.enter_context(tc.tile_pool(name="ordered_pool", bufs=3))
+        ordered_pool = ctx.enter_context(tc.tile_pool(name="ordered_pool", bufs=6))
         work = ctx.enter_context(tc.tile_pool(name="work", bufs=6))
         uv_pool = ctx.enter_context(tc.tile_pool(name="uv_pool", bufs=GROUPS))
         psum_t = ctx.enter_context(tc.psum_pool(name="psum_t", bufs=4))
@@ -45,12 +43,24 @@ def tile_retentionmechanism_pa_t_kernel(tc, y, w_swiglu_words, w_swiglu_scales, 
         identity = consts.tile([P, P], F32)
         make_identity(nc, identity[:])
 
+        seen = consts.tile([P, 1], U32)
         w_codes = consts.tile([P, 2 * WIDTH], U32, align_bytes=64)
         w_scales = consts.tile([P, 2 * WIDTH], U8, align_bytes=64)
         nc.vector.memset(w_scales[:].bitcast(I32), 0)
 
+        rounds = [[g, g + 1] for g in range(0, GROUPS, 2)]
+        last = len(rounds)
+        reordered = {(2 * r + 1, b) for r in range(2, last) for b in range(2) if b == 1 or r % 2 == 0}
+
         y_tiles, y_ordered, y_grouped, y_codes, y_scales = {}, {}, {}, {}, {}
+        y_first = []
         t_banks, m_banks, uv_grouped, uv_codes, uv_scales = {}, {}, {}, {}, {}
+
+        def load_first_group():
+            for b in range(2):
+                half = consts.tile([P, 2 * FEATURES], BF16, name=f"y_first_{b}")
+                nc.sync.dma_start(out=half[:], in_=y_groups[0][:, 2 * FEATURES * b : 2 * FEATURES * (b + 1)])
+                y_first.append(half)
 
         def load_group(g):
             y_tiles[g] = y_pool.tile([P, PACK * FEATURES], BF16, name="y_sb")
@@ -67,26 +77,31 @@ def tile_retentionmechanism_pa_t_kernel(tc, y, w_swiglu_words, w_swiglu_scales, 
                     in_=w_swiglu_scales[0, r:16:4, :].bitcast(I32),
                 )
 
-        def order_group(g):
-            y_ordered[g] = ordered_pool.tile([P, PACK * WORDS], F32, name="y_ordered")
-            for half in range(2):
-                columns = slice(2 * WORDS * half, 2 * WORDS * (half + 1))
-                nc.gpsimd.tensor_copy(
-                    out=y_ordered[g][:, columns].rearrange("p (j u c) -> p j u c", j=2, u=2),
-                    in_=y_tiles[g][:].bitcast(F32)[:, columns].rearrange("p (j c u) -> p j u c", j=2, u=2),
-                )
+        def wait_for_vector(g):
+            nc.gpsimd.tensor_copy(out=seen[:], in_=uv_codes[g][:, 0:1])
 
-        def word_columns(g, j, u):
-            if g in y_ordered:
-                return y_ordered[g][:, WORDS * j + P * u : WORDS * j + P * (u + 1)]
+        def reorder(g, b):
+            y_ordered[(g, b)] = ordered_pool.tile([P, 2 * WORDS], F32, name="y_ordered")
+            nc.gpsimd.tensor_copy(
+                out=y_ordered[(g, b)][:].rearrange("p (j u c) -> p j u c", j=2, u=2),
+                in_=y_tiles[g][:].bitcast(F32)[:, 2 * WORDS * b : 2 * WORDS * (b + 1)].rearrange(
+                    "p (j c u) -> p j u c", j=2, u=2
+                ),
+            )
+
+        def word_columns(g, b, a, u):
+            if (g, b) in reordered:
+                return y_ordered[(g, b)][:, WORDS * a + P * u : WORDS * a + P * (u + 1)]
+            if g == 0:
+                return y_first[b][:].bitcast(F32)[:, WORDS * a + u : WORDS * (a + 1) : 2]
+            j = 2 * b + a
             return y_tiles[g][:].bitcast(F32)[:, WORDS * j + u : WORDS * (j + 1) : 2]
 
         def transpose_bank(g, b):
             bank = psum_t.tile([P, 2, 2, P], F32, name="bank_t")
             for a in range(2):
-                j = 2 * b + a
                 for u in range(2):
-                    nc.tensor.transpose(bank[:, a, u, :], word_columns(g, j, u), identity[:])
+                    nc.tensor.transpose(bank[:, a, u, :], word_columns(g, b, a, u), identity[:])
             t_banks[(g, b)] = bank
 
         def copy_t(copy, g, b):
@@ -153,46 +168,44 @@ def tile_retentionmechanism_pa_t_kernel(tc, y, w_swiglu_words, w_swiglu_scales, 
 
         s_copy, v_copy = nc.scalar.copy, nc.vector.tensor_copy
 
-        for g in range(Y_BUFFERS):
+        load_first_group()
+        load_group(1)
+        load_w()
+        for g in range(2, Y_BUFFERS):
             load_group(g)
-            if g == 3:
-                load_w()
 
-        for r in range(ROUNDS + 3):
-            now = [PER_ROUND * r + i for i in range(PER_ROUND)]
-            one = [g - PER_ROUND for g in now]
-            two = [g - 2 * PER_ROUND for g in now]
-            three = [g - 3 * PER_ROUND for g in now]
-            if r < ROUNDS:
-                for g in now:
-                    for b in range(2):
-                        transpose_bank(g, b)
-                    if g + Y_BUFFERS < GROUPS:
-                        load_group(g + Y_BUFFERS)
-            if 2 <= r < ROUNDS + 2:
-                copy_m(s_copy, two[0], 0)
-                copy_m(v_copy, two[0], 1)
-                copy_m(s_copy, two[1], 0)
-                copy_m(s_copy, two[1], 1)
-            if 1 <= r < ROUNDS + 1:
-                for g in one:
-                    quantise_y(g)
-                for g in one:
-                    first_product(g)
-            if r % 2 == 0 and r + 2 < ROUNDS:
-                order_group(PER_ROUND * (r + 2) + 1)
-            if r < ROUNDS:
-                copy_t(s_copy, now[0], 0)
-                copy_t(s_copy, now[0], 1)
-                copy_t(v_copy, now[1], 0)
-                copy_t(v_copy if r % 4 == 3 else s_copy, now[1], 1)
-            if r >= 3:
-                for g in three:
-                    quantise_uv(g)
-            if r == ROUNDS - 1:
+        for r in range(last + 3):
+            now, one, two, three = (
+                rounds[r - lag] if 0 <= r - lag < last else [] for lag in range(4)
+            )
+            for g in now:
+                for b in range(2):
+                    transpose_bank(g, b)
+                if g + Y_BUFFERS < GROUPS:
+                    load_group(g + Y_BUFFERS)
+            if r == last:
                 result = psum_t.tile([P, 2, 2, P], F32, name="bank_t")[:, 0, 0, :]
                 for g in range(GROUPS // 2):
                     second_product(g)
+            for g in one:
+                quantise_y(g)
+            for g in three:
+                quantise_uv(g)
+            if r + 2 < last:
+                if three:
+                    wait_for_vector(three[-1])
+                for g in rounds[r + 2]:
+                    for b in range(2):
+                        if (g, b) in reordered:
+                            reorder(g, b)
+            for i, g in enumerate(two):
+                copy_m(s_copy, g, 0)
+                copy_m(v_copy if i == 1 else s_copy, g, 1)
+            for g in one:
+                first_product(g)
+            for i, g in enumerate(now):
+                copy_t(v_copy if i == 1 else s_copy, g, 0)
+                copy_t(s_copy, g, 1)
         for g in range(GROUPS // 2, GROUPS):
             second_product(g)
 

@@ -20,6 +20,7 @@ ALL_TOKENS = BATCH * TOKENS
 GROUPS = ALL_TOKENS // K_PASS
 WORDS = FEATURES // 2
 Y_BUFFERS = 8
+EARLY = 12
 
 FLOPS = 2 * ALL_TOKENS * FEATURES * 2 * WIDTH + 2 * ALL_TOKENS * WIDTH * WIDTH
 
@@ -34,7 +35,7 @@ def tile_retentionmechanism_pa_t_kernel(tc, y, w_swiglu_words, w_swiglu_scales, 
         ctx.enter_context(tc.manual_schedule())
         consts = ctx.enter_context(tc.tile_pool(name="consts", bufs=1))
         y_pool = ctx.enter_context(tc.tile_pool(name="y_pool", bufs=Y_BUFFERS))
-        ordered_pool = ctx.enter_context(tc.tile_pool(name="ordered_pool", bufs=6))
+        ordered_pool = ctx.enter_context(tc.tile_pool(name="ordered_pool", bufs=3))
         work = ctx.enter_context(tc.tile_pool(name="work", bufs=6))
         uv_pool = ctx.enter_context(tc.tile_pool(name="uv_pool", bufs=GROUPS))
         psum_t = ctx.enter_context(tc.psum_pool(name="psum_t", bufs=4))
@@ -43,14 +44,13 @@ def tile_retentionmechanism_pa_t_kernel(tc, y, w_swiglu_words, w_swiglu_scales, 
         identity = consts.tile([P, P], F32)
         make_identity(nc, identity[:])
 
-        seen = consts.tile([P, 1], U32)
         w_codes = consts.tile([P, 2 * WIDTH], U32, align_bytes=64)
         w_scales = consts.tile([P, 2 * WIDTH], U8, align_bytes=64)
         nc.vector.memset(w_scales[:].bitcast(I32), 0)
 
         rounds = [[g, g + 1] for g in range(0, GROUPS, 2)]
         last = len(rounds)
-        reordered = {(2 * r + 1, b) for r in range(2, last) for b in range(2) if b == 1 or r % 2 == 0}
+        reordered = {(2 * r + 1, 1) for r in range(2, last - 2, 2)}
 
         y_tiles, y_ordered, y_grouped, y_codes, y_scales = {}, {}, {}, {}, {}
         y_first = []
@@ -77,12 +77,9 @@ def tile_retentionmechanism_pa_t_kernel(tc, y, w_swiglu_words, w_swiglu_scales, 
                     in_=w_swiglu_scales[0, r:16:4, :].bitcast(I32),
                 )
 
-        def wait_for_vector(g):
-            nc.gpsimd.tensor_copy(out=seen[:], in_=uv_codes[g][:, 0:1])
-
         def reorder(g, b):
             y_ordered[(g, b)] = ordered_pool.tile([P, 2 * WORDS], F32, name="y_ordered")
-            nc.gpsimd.tensor_copy(
+            nc.vector.tensor_copy(
                 out=y_ordered[(g, b)][:].rearrange("p (j u c) -> p j u c", j=2, u=2),
                 in_=y_tiles[g][:].bitcast(F32)[:, 2 * WORDS * b : 2 * WORDS * (b + 1)].rearrange(
                     "p (j c u) -> p j u c", j=2, u=2
@@ -185,28 +182,25 @@ def tile_retentionmechanism_pa_t_kernel(tc, y, w_swiglu_words, w_swiglu_scales, 
                     load_group(g + Y_BUFFERS)
             if r == last:
                 result = psum_t.tile([P, 2, 2, P], F32, name="bank_t")[:, 0, 0, :]
-                for g in range(GROUPS // 2):
+                for g in range(EARLY):
                     second_product(g)
             for g in one:
                 quantise_y(g)
             for g in three:
                 quantise_uv(g)
-            if r + 2 < last:
-                if three:
-                    wait_for_vector(three[-1])
-                for g in rounds[r + 2]:
-                    for b in range(2):
-                        if (g, b) in reordered:
-                            reorder(g, b)
             for i, g in enumerate(two):
                 copy_m(s_copy, g, 0)
                 copy_m(v_copy if i == 1 else s_copy, g, 1)
             for g in one:
                 first_product(g)
+            for g in rounds[r + 1] if r + 1 < last else []:
+                for b in range(2):
+                    if (g, b) in reordered:
+                        reorder(g, b)
             for i, g in enumerate(now):
                 copy_t(v_copy if i == 1 else s_copy, g, 0)
-                copy_t(s_copy, g, 1)
-        for g in range(GROUPS // 2, GROUPS):
+                copy_t(v_copy if i == 1 and r % 4 == 0 else s_copy, g, 1)
+        for g in range(EARLY, GROUPS):
             second_product(g)
 
         scaled = consts.tile([P, WIDTH], F32)

from contextlib import ExitStack
import math

import concourse.mybir as mybir
from concourse.masks import make_identity

F32 = mybir.dt.float32
BF16 = mybir.dt.bfloat16
I32 = mybir.dt.int32
U32 = mybir.dt.uint32
U8 = mybir.dt.uint8
FP8X4 = mybir.dt.float8_e4m3fn_x4

P = 128
PACK = 4
K_PASS = P * PACK

BATCH, TOKENS, FEATURES, WIDTH = 4, 4096, 512, 128
ALL_TOKENS = BATCH * TOKENS
GROUPS = ALL_TOKENS // K_PASS
WORDS = FEATURES // 2
Y_BUFFERS = 8
EARLY = 12

FLOPS = 2 * ALL_TOKENS * FEATURES * 2 * WIDTH + 2 * ALL_TOKENS * WIDTH * WIDTH


def tile_retentionmechanism_pa_t_kernel(tc, y, w_swiglu_words, w_swiglu_scales, out):
    nc = tc.nc
    assert FEATURES == K_PASS

    y_groups = y.rearrange("b t q -> (b t) q").rearrange("(g p j) q -> g p (j q)", p=P, j=PACK)

    with ExitStack() as ctx:
        ctx.enter_context(tc.manual_schedule())
        consts = ctx.enter_context(tc.tile_pool(name="consts", bufs=1))
        y_pool = ctx.enter_context(tc.tile_pool(name="y_pool", bufs=Y_BUFFERS))
        ordered_pool = ctx.enter_context(tc.tile_pool(name="ordered_pool", bufs=3))
        work = ctx.enter_context(tc.tile_pool(name="work", bufs=6))
        uv_pool = ctx.enter_context(tc.tile_pool(name="uv_pool", bufs=GROUPS))
        psum_t = ctx.enter_context(tc.psum_pool(name="psum_t", bufs=4))
        psum_m = ctx.enter_context(tc.psum_pool(name="psum_m", bufs=4))

        identity = consts.tile([P, P], F32)
        make_identity(nc, identity[:])

        w_codes = consts.tile([P, 2 * WIDTH], U32, align_bytes=64)
        w_scales = consts.tile([P, 2 * WIDTH], U8, align_bytes=64)
        nc.vector.memset(w_scales[:].bitcast(I32), 0)

        rounds = [[g, g + 1] for g in range(0, GROUPS, 2)]
        last = len(rounds)
        reordered = {(2 * r + 1, 1) for r in range(2, last - 2, 2)}

        y_tiles, y_ordered, y_grouped, y_codes, y_scales = {}, {}, {}, {}, {}
        y_first = []
        t_banks, m_banks, uv_grouped, uv_codes, uv_scales = {}, {}, {}, {}, {}

        def load_first_group():
            for b in range(2):
                half = consts.tile([P, 2 * FEATURES], BF16, name=f"y_first_{b}")
                nc.sync.dma_start(out=half[:], in_=y_groups[0][:, 2 * FEATURES * b : 2 * FEATURES * (b + 1)])
                y_first.append(half)

        def load_group(g):
            y_tiles[g] = y_pool.tile([P, PACK * FEATURES], BF16, name="y_sb")
            nc.sync.dma_start(out=y_tiles[g][:], in_=y_groups[g])

        def load_w():
            nc.sync.dma_start(
                out=w_codes[:].bitcast(I32),
                in_=w_swiglu_words.rearrange("g p n t -> (g p) (n t)").bitcast(I32),
            )
            for r in range(4):
                nc.sync.dma_start(
                    out=w_scales[r:P:32, :].bitcast(I32),
                    in_=w_swiglu_scales[0, r:16:4, :].bitcast(I32),
                )

        def reorder(g, b):
            y_ordered[(g, b)] = ordered_pool.tile([P, 2 * WORDS], F32, name="y_ordered")
            nc.vector.tensor_copy(
                out=y_ordered[(g, b)][:].rearrange("p (j u c) -> p j u c", j=2, u=2),
                in_=y_tiles[g][:].bitcast(F32)[:, 2 * WORDS * b : 2 * WORDS * (b + 1)].rearrange(
                    "p (j c u) -> p j u c", j=2, u=2
                ),
            )

        def word_columns(g, b, a, u):
            if (g, b) in reordered:
                return y_ordered[(g, b)][:, WORDS * a + P * u : WORDS * a + P * (u + 1)]
            if g == 0:
                return y_first[b][:].bitcast(F32)[:, WORDS * a + u : WORDS * (a + 1) : 2]
            j = 2 * b + a
            return y_tiles[g][:].bitcast(F32)[:, WORDS * j + u : WORDS * (j + 1) : 2]

        def transpose_bank(g, b):
            bank = psum_t.tile([P, 2, 2, P], F32, name="bank_t")
            for a in range(2):
                for u in range(2):
                    nc.tensor.transpose(bank[:, a, u, :], word_columns(g, b, a, u), identity[:])
            t_banks[(g, b)] = bank

        def copy_t(copy, g, b):
            if b == 0:
                y_grouped[g] = work.tile([P, PACK * K_PASS], BF16, name="y_grouped", align_bytes=64)
            copy(
                out=y_grouped[g][:].bitcast(F32)[:, 4 * P * b : 4 * P * (b + 1)].rearrange(
                    "p (a r u) -> p a r u", a=2, u=2
                ),
                in_=t_banks[(g, b)][:].rearrange("p a u r -> p a r u"),
            )

        def quantise_y(g):
            y_codes[g] = work.tile([P, K_PASS], U32, name="y_codes", align_bytes=64)
            y_scales[g] = work.tile([P, K_PASS], U8, name="y_scales", align_bytes=64)
            nc.vector.quantize_mx(
                out=y_codes[g][:].bitcast(FP8X4), scales=y_scales[g][:], in_=y_grouped[g][:]
            )

        def first_product(g):
            for half in range(2):
                columns = slice(WIDTH * half, WIDTH * (half + 1))
                bank = psum_m.tile([P, PACK, WIDTH], F32, name="bank_m")
                for j in range(PACK):
                    tokens = slice(P * j, P * (j + 1))
                    nc.tensor.matmul_mx(
                        out=bank[:, j, :],
                        lhsT=y_codes[g][:, tokens].bitcast(FP8X4),
                        lhsT_scale=y_scales[g][:, tokens],
                        rhs=w_codes[:, columns].bitcast(FP8X4),
                        rhs_scale=w_scales[:, columns],
                        start=True,
                        stop=True,
                    )
                m_banks[(g, half)] = bank

        def copy_m(copy, g, half):
            if half == 0:
                uv_grouped[g] = work.tile([P, 2 * WIDTH, PACK], BF16, name="uv_grouped", align_bytes=64)
            copy(
                out=uv_grouped[g][:, WIDTH * half : WIDTH * (half + 1), :],
                in_=m_banks[(g, half)][:].rearrange("p j w -> p w j"),
            )

        def quantise_uv(g):
            uv_codes[g] = uv_pool.tile([P, 2 * WIDTH], U32, name="uv_codes", align_bytes=64)
            uv_scales[g] = uv_pool.tile([P, 2 * WIDTH], U8, name="uv_scales", align_bytes=64)
            nc.vector.quantize_mx(
                out=uv_codes[g][:].bitcast(FP8X4),
                scales=uv_scales[g][:],
                in_=uv_grouped[g][:].rearrange("p w j -> p (w j)"),
            )

        def second_product(g):
            nc.tensor.matmul_mx(
                out=result,
                lhsT=uv_codes[g][:, 0:WIDTH].bitcast(FP8X4),
                lhsT_scale=uv_scales[g][:, 0:WIDTH],
                rhs=uv_codes[g][:, WIDTH : 2 * WIDTH].bitcast(FP8X4),
                rhs_scale=uv_scales[g][:, WIDTH : 2 * WIDTH],
                start=(g == 0),
                stop=(g == GROUPS - 1),
            )

        s_copy, v_copy = nc.scalar.copy, nc.vector.tensor_copy

        load_first_group()
        load_group(1)
        load_w()
        for g in range(2, Y_BUFFERS):
            load_group(g)

        for r in range(last + 3):
            now, one, two, three = (
                rounds[r - lag] if 0 <= r - lag < last else [] for lag in range(4)
            )
            for g in now:
                for b in range(2):
                    transpose_bank(g, b)
                if g + Y_BUFFERS < GROUPS:
                    load_group(g + Y_BUFFERS)
            if r == last:
                result = psum_t.tile([P, 2, 2, P], F32, name="bank_t")[:, 0, 0, :]
                for g in range(EARLY):
                    second_product(g)
            for g in one:
                quantise_y(g)
            for g in three:
                quantise_uv(g)
            for i, g in enumerate(two):
                copy_m(s_copy, g, 0)
                copy_m(v_copy if i == 1 else s_copy, g, 1)
            for g in one:
                first_product(g)
            for g in rounds[r + 1] if r + 1 < last else []:
                for b in range(2):
                    if (g, b) in reordered:
                        reorder(g, b)
            for i, g in enumerate(now):
                copy_t(v_copy if i == 1 else s_copy, g, 0)
                copy_t(v_copy if i == 1 and r % 4 == 0 else s_copy, g, 1)
        for g in range(EARLY, GROUPS):
            second_product(g)

        scaled = consts.tile([P, WIDTH], F32)
        nc.vector.tensor_scalar_mul(out=scaled[:], in0=result, scalar1=1.0 / BATCH / math.sqrt(WIDTH))
        nc.sync.dma_start(out=out, in_=scaled[:])
